import numpy as np
import ml_dtypes


def mxq(x, axis, fmt="e4m3"):
    dtype, down = {"e4m3": (ml_dtypes.float8_e4m3fn, 7), "e5m2": (ml_dtypes.float8_e5m2, 14)}[fmt]
    v = np.moveaxis(np.asarray(x, np.float32).astype(ml_dtypes.bfloat16).astype(np.float64), axis, -1)
    blocks = v.reshape(v.shape[:-1] + (-1, 32))
    amax = np.abs(blocks).max(-1, keepdims=True)
    byte = np.maximum(np.where(amax > 0, np.frexp(amax)[1] - 1 + 127, 0) - down, 1)
    scale = np.exp2(byte - 127.0)
    codes = (blocks / scale).astype(np.float32).astype(dtype).astype(np.float64)
    return np.moveaxis((codes * scale).reshape(v.shape), -1, axis)


WIDE = False


def mx_kscale(k):
    if not WIDE:
        return np.ones(k)
    levels = np.array([10, -10, 5, -5, 0])
    a = np.random.permutation(np.resize(levels, k // 512 * 4)).reshape(k // 512, 4)
    idx = np.arange(k)
    return np.exp2(a[idx // 512, idx % 128 // 32])


BF16 = ml_dtypes.bfloat16


def bf(x):
    return np.asarray(x, np.float32).astype(BF16)


def f64(x):
    return np.asarray(x).astype(np.float64)


B, IN_DIM, MEM = 512, 16128, 256
DIN = MEM + IN_DIM
MIN_TS, MAX_TS, EPS = 0.1, 10.0, 1e-6


def sigmoid(v):
    return 1.0 / (1.0 + np.exp(-v))


def setup_inputs():
    s = mx_kscale(DIN)[MEM:]
    r = np.concatenate([np.ones(MEM), s])
    return {"x": bf(np.random.standard_normal((B, IN_DIM)) * s),
            "h": bf(np.random.standard_normal((B, MEM))),
            "h_candidate": bf(np.tanh(0.7 * np.random.standard_normal((B, MEM)))),
            "Wd": bf(np.random.standard_normal((DIN, MEM)) * 1.3 / np.sqrt(DIN) / r[:, None]),
            "bd": bf(np.random.standard_normal(MEM) * 0.5),
            "Wu": bf(np.random.standard_normal((DIN, MEM)) * 1.3 / np.sqrt(DIN) / r[:, None]),
            "bu": bf(np.random.standard_normal(MEM) * 0.5)}


def reference(x, h, h_candidate, Wd, bd, Wu, bu):
    h = f64(h)
    cq = mxq(np.concatenate([h, f64(x)], axis=-1), 1, "e4m3")
    decay = sigmoid((cq @ mxq(f64(Wd), 0, "e4m3")) + f64(bd))
    update = sigmoid((cq @ mxq(f64(Wu), 0, "e4m3")) + f64(bu))
    decay = MIN_TS + (MAX_TS - MIN_TS) * decay + EPS
    new_h = (1.0 - update) * (h / decay) + update * f64(h_candidate)
    h_norm = np.maximum(np.sqrt(np.square(h).sum(-1, keepdims=True)), EPS)
    nh_norm = np.maximum(np.sqrt(np.square(new_h).sum(-1, keepdims=True)), 1e-12)
    return new_h / nh_norm * h_norm

@@ -1,0 +1,276 @@
+import math
+from contextlib import ExitStack
+
+import concourse.mybir as mybir
+from concourse.masks import make_identity
+
+F32 = mybir.dt.float32
+BF16 = mybir.dt.bfloat16
+U32 = mybir.dt.uint32
+U8 = mybir.dt.uint8
+FP8X4 = mybir.dt.float8_e4m3fn_x4
+ALU = mybir.AluOpType
+ACT = mybir.ActivationFunctionType
+
+BATCH, IN_DIM, MEM = 512, 16128, 256
+K = MEM + IN_DIM
+P = 128
+K_PASS = 4 * P
+PASSES = K // K_PASS
+CHUNK = 4
+CHUNKS = PASSES // CHUNK
+B_TILES = BATCH // P
+UNITS = CHUNKS * B_TILES
+UNIT_COLS = CHUNK * K_PASS
+N_OUT = 2 * MEM
+
+ROW_ORDER_CHUNKS = 1
+W_LEAD = 3
+AHEAD = 6
+C_BUFS = AHEAD
+W_BUFS = (AHEAD + 2) // 2
+V_COLS = 160
+
+MIN_TS, MAX_TS, EPS = 0.1, 10.0, 1e-6
+SPAN = MAX_TS - MIN_TS
+DECAY_LO = MIN_TS + EPS
+DECAY_HI = DECAY_LO + SPAN
+INV_HI = 1.0 / DECAY_HI
+INV_SPAN = SPAN / (DECAY_LO * DECAY_HI)
+SHIFT = math.log(DECAY_HI / DECAY_LO)
+
+FLOPS = 2 * BATCH * K * N_OUT
+
+
+def tile_liquidmemorycell_pb_k_kernel(tc, x, h, h_candidate, Wd, bd, Wu, bu, out):
+    nc = tc.nc
+    weights = (Wd, Wu)
+    with ExitStack() as ctx:
+        consts = ctx.enter_context(tc.tile_pool(name="consts", bufs=1))
+        c_pool = ctx.enter_context(tc.tile_pool(name="c_raw", bufs=C_BUFS))
+        w_pool = ctx.enter_context(tc.tile_pool(name="w_raw", bufs=W_BUFS))
+        grouped = ctx.enter_context(tc.tile_pool(name="grouped", bufs=3))
+        w_mx = ctx.enter_context(tc.tile_pool(name="w_mx", bufs=W_LEAD + CHUNK + 1))
+        c_mx = ctx.enter_context(tc.tile_pool(name="c_mx", bufs=3))
+        tail = ctx.enter_context(tc.tile_pool(name="tail", bufs=3))
+        acc_pool = ctx.enter_context(tc.psum_pool(name="acc", bufs=1))
+        xt_pool = ctx.enter_context(tc.psum_pool(name="xt", bufs=4))
+        ctx.enter_context(tc.manual_schedule())
+
+        c_raw, w_raw, w_grouped, w_codes, w_scales = {}, {}, {}, {}, {}
+        c_banks, c_grouped, c_codes, c_scales = {}, {}, {}, {}
+        gate, blend, ratios = {}, {}, {}
+
+        def load_unit(n):
+            ci, b = divmod(n, B_TILES)
+            rows = slice(b * P, (b + 1) * P)
+            raw = c_pool.tile([P, UNIT_COLS], BF16, name="c_raw")
+            if ci == 0:
+                nc.sync.dma_start(out=raw[:, 0:MEM], in_=h[rows, :])
+                nc.sync.dma_start(out=raw[:, MEM:], in_=x[rows, 0 : UNIT_COLS - MEM])
+            else:
+                first = ci * UNIT_COLS - MEM
+                nc.sync.dma_start(out=raw[:], in_=x[rows, first : first + UNIT_COLS])
+            c_raw[n] = raw
+
+        def load_weight_pair(q):
+            rows = slice(2 * q * K_PASS, (2 * q + 2) * K_PASS)
+            raw = w_pool.tile([P, 2, 2, 4, MEM], BF16, name="w_raw")
+            for w in range(2):
+                if (2 * q) // CHUNK < ROW_ORDER_CHUNKS:
+                    nc.sync.dma_start(
+                        out=raw[:, w].rearrange("p g t n -> p g (t n)"),
+                        in_=weights[w][rows, :].rearrange("(g p t) n -> p g (t n)", g=2, t=4),
+                    )
+                else:
+                    nc.sync.dma_start(
+                        out=raw[:, w].rearrange("p g (u e) n -> p (g u) (e n)", e=2),
+                        in_=weights[w][rows, :].rearrange("(s p e) n -> p s (e n)", s=4, e=2),
+                    )
+            w_raw[q] = raw
+
+        def regroup_weights(pn):
+            raw = w_raw[pn // 2]
+            g = pn % 2
+            gw = grouped.tile([P, 2, MEM, 4], BF16, name="gw", align_bytes=64)
+            nc.vector.tensor_copy(
+                out=gw[:, :, 0:V_COLS, :].rearrange("p w (c i) t -> p w c t i", i=4),
+                in_=raw[:, :, g, :, 0:V_COLS].rearrange("p w t (c i) -> p w c t i", i=4),
+            )
+            for w in range(2):
+                nc.scalar.copy(
+                    out=gw[:, w, V_COLS:, :].rearrange("p (c i) t -> p c t i", i=4),
+                    in_=raw[:, w, g, :, V_COLS:].rearrange("p t (c i) -> p c t i", i=4),
+                )
+            w_grouped[pn] = gw
+
+        def quantise_weights(pn):
+            codes = w_mx.tile([P, N_OUT], U32, name="w_codes", align_bytes=64)
+            scales = w_mx.tile([P, N_OUT], U8, name="w_scales", align_bytes=64)
+            nc.vector.quantize_mx(
+                out=codes[:].bitcast(FP8X4),
+                scales=scales[:],
+                in_=w_grouped[pn][:].rearrange("p w n t -> p (w n t)"),
+            )
+            w_codes[pn], w_scales[pn] = codes, scales
+
+        def transpose_unit(n):
+            ci = n // B_TILES
+            words = c_raw[n][:].bitcast(F32)
+            if ci < ROW_ORDER_CHUNKS:
+                planes = words.rearrange("r (g p u) -> r g u p", g=CHUNK, u=2)
+            else:
+                planes = words.rearrange("r (g u p) -> r g u p", g=CHUNK, u=2)
+            banks = []
+            for half in range(2):
+                xt = xt_pool.tile([P, 4, P], F32, name="xt")
+                for j in range(4):
+                    nc.tensor.transpose(xt[:, j, :], planes[:, 2 * half + j // 2, j % 2, :], ident[:])
+                banks.append(xt)
+            c_banks[n] = banks
+
+        def copy_out_unit(n):
+            gx = grouped.tile([P, UNIT_COLS], BF16, name="gx", align_bytes=64)
+            gx_words = gx[:].bitcast(F32).rearrange("p (f g r u) -> p f g r u", f=2, g=2, u=2)
+            for half in range(2):
+                nc.scalar.copy(
+                    out=gx_words[:, half],
+                    in_=c_banks[n][half][:].rearrange("p (g u) r -> p g r u", u=2),
+                )
+            c_grouped[n] = gx
+
+        def quantise_unit(n):
+            codes = c_mx.tile([P, CHUNK * P], U32, name="c_codes", align_bytes=64)
+            scales = c_mx.tile([P, CHUNK * P], U8, name="c_scales", align_bytes=64)
+            nc.vector.quantize_mx(out=codes[:].bitcast(FP8X4), scales=scales[:], in_=c_grouped[n][:])
+            c_codes[n], c_scales[n] = codes, scales
+
+        def multiply_unit(n):
+            ci, b = divmod(n, B_TILES)
+            for g in range(CHUNK):
+                pn = ci * CHUNK + g
+                rows = slice(g * P, (g + 1) * P)
+                nc.tensor.matmul_mx(
+                    out=acc[b][:],
+                    lhsT=c_codes[n][:, rows].bitcast(FP8X4),
+                    lhsT_scale=c_scales[n][:, rows],
+                    rhs=w_codes[pn][:].bitcast(FP8X4),
+                    rhs_scale=w_scales[pn][:],
+                    start=(pn == 0),
+                    stop=(pn == PASSES - 1),
+                )
+
+        def prepare_from_h(b):
+            h_cols = c_raw[b][:, 0:MEM]
+            square = tail.tile([P, MEM], F32, name="square")
+            nc.scalar.activation(out=h_span[:, b, :], in_=h_cols, func=ACT.Copy, scale=INV_SPAN)
+            nc.scalar.activation(out=square[:], in_=h_cols, func=ACT.Square, accum_out=h_sq[:, b : b + 1])
+            nc.vector.scalar_tensor_tensor(
+                out=rest[:, b, :], in0=h_cols, scalar=INV_HI, in1=cand[:, b, :], op0=ALU.mult, op1=ALU.subtract
+            )
+
+        def gates(b):
+            z = tail.tile([P, N_OUT], F32, name="z")
+            s = tail.tile([P, N_OUT], F32, name="s")
+            for cols in (slice(0, MEM), slice(MEM, N_OUT)):
+                nc.vector.tensor_tensor(out=z[:, cols], in0=acc[b][:, cols], in1=bias_all[:, cols], op=ALU.add)
+                nc.scalar.activation(out=s[:, cols], in_=z[:, cols], func=ACT.Sigmoid, scale=-1.0)
+            gate[b] = s
+
+        def mix(b):
+            s = gate[b]
+            m = tail.tile([P, MEM], F32, name="m")
+            nc.vector.tensor_tensor(out=m[:], in0=s[:, 0:MEM], in1=h_span[:, b, :], op=ALU.mult)
+            nc.vector.tensor_tensor(out=m[:], in0=m[:], in1=rest[:, b, :], op=ALU.add)
+            nc.vector.tensor_tensor(out=m[:], in0=m[:], in1=s[:, MEM:], op=ALU.mult)
+            nc.vector.tensor_tensor(out=m[:], in0=m[:], in1=cand[:, b, :], op=ALU.add)
+            blend[b] = m
+
+        def norm_ratio(b):
+            square = tail.tile([P, MEM], F32, name="square")
+            m_sq = tail.tile([P, 1], F32, name="m_sq")
+            nc.scalar.activation(out=square[:], in_=blend[b][:], func=ACT.Square, accum_out=m_sq[:])
+            ratio = tail.tile([P, 1], F32, name="ratio")
+            nc.gpsimd.tensor_scalar(out=ratio[:], in0=m_sq[:], scalar1=1e-24, scalar2=None, op0=ALU.max)
+            nc.gpsimd.tensor_tensor(out=ratio[:], in0=ratio[:], in1=minus_half[:], op=ALU.pow)
+            nc.gpsimd.tensor_tensor(out=ratio[:], in0=ratio[:], in1=h_norm[:, b : b + 1], op=ALU.mult)
+            ratios[b] = ratio
+
+        def store_tile(b):
+            result = tail.tile([P, MEM], F32, name="result")
+            nc.scalar.activation(out=result[:], in_=blend[b][:], func=ACT.Copy, scale=ratios[b][:])
+            nc.sync.dma_start(out=out[b * P : (b + 1) * P, :], in_=result[:])
+
+        def load_round(j):
+            if (j + W_LEAD) % 2 == 0 and j + W_LEAD < PASSES:
+                load_weight_pair((j + W_LEAD) // 2)
+            load_unit(j)
+
+        ident = consts.tile([P, P], F32, name="ident")
+        make_identity(nc, ident[:])
+        plus_half = consts.tile([P, B_TILES], F32, name="plus_half")
+        nc.gpsimd.memset(plus_half[:], 0.5)
+        minus_half = consts.tile([P, 1], F32, name="minus_half")
+        nc.gpsimd.memset(minus_half[:], -0.5)
+
+        ones = consts.tile([P, P], BF16, name="ones")
+        nc.vector.memset(ones[:], 1.0)
+        bias_row = consts.tile([P, N_OUT], BF16, name="bias_row")
+        nc.vector.memset(bias_row[:], 0.0)
+        warm = consts.tile([P, 1], F32, name="warm")
+        nc.vector.memset(warm[:], 0.0)
+        nc.scalar.activation(out=warm[:], in_=warm[:], func=ACT.Sigmoid)
+
+        nc.sync.dma_start(out=bias_row[0:1, 0:MEM], in_=bd.rearrange("(o n) -> o n", o=1))
+        nc.sync.dma_start(out=bias_row[0:1, MEM:], in_=bu.rearrange("(o n) -> o n", o=1))
+        for q in range((W_LEAD + 1) // 2):
+            load_weight_pair(q)
+        cand = consts.tile([P, B_TILES, MEM], BF16, name="cand")
+        nc.sync.dma_start(out=cand[:], in_=h_candidate.rearrange("(b p) n -> p b n", p=P))
+        for j in range(AHEAD):
+            load_round(j)
+
+        bias_bank = xt_pool.tile([P, N_OUT], F32, name="xt")
+        nc.tensor.matmul(out=bias_bank[:], lhsT=ones[:], rhs=bias_row[:], start=True, stop=True)
+        bias_all = consts.tile([P, N_OUT], F32, name="bias_all")
+        nc.vector.tensor_scalar_add(out=bias_all[:, 0:MEM], in0=bias_bank[:, 0:MEM], scalar1=SHIFT)
+        nc.vector.tensor_copy(out=bias_all[:, MEM:], in_=bias_bank[:, MEM:])
+
+        h_span = consts.tile([P, B_TILES, MEM], F32, name="h_span")
+        rest = consts.tile([P, B_TILES, MEM], F32, name="rest")
+        h_sq = consts.tile([P, B_TILES], F32, name="h_sq")
+        h_norm = consts.tile([P, B_TILES], F32, name="h_norm")
+        acc = []
+        for b in range(B_TILES):
+            bank = acc_pool.tile([P, N_OUT], F32, name="acc%d" % b)
+            acc.append(bank)
+
+        for i in range(-W_LEAD, UNITS + 3):
+            pn = i + W_LEAD
+            b = i - 1 - (UNITS - B_TILES)
+            if 1 <= pn <= PASSES:
+                quantise_weights(pn - 1)
+            if 0 <= i < UNITS:
+                transpose_unit(i)
+            if 1 <= i <= UNITS:
+                multiply_unit(i - 1)
+            if 0 <= i < UNITS:
+                copy_out_unit(i)
+            if 0 <= i < B_TILES:
+                prepare_from_h(i)
+            if i == B_TILES:
+                nc.gpsimd.tensor_scalar(out=h_norm[:], in0=h_sq[:], scalar1=1e-12, scalar2=None, op0=ALU.max)
+                nc.gpsimd.tensor_tensor(out=h_norm[:], in0=h_norm[:], in1=plus_half[:], op=ALU.pow)
+            if 0 <= b - 2 < B_TILES:
+                store_tile(b - 2)
+            if 0 <= b - 1 < B_TILES:
+                norm_ratio(b - 1)
+            if pn < PASSES:
+                regroup_weights(pn)
+            if 0 <= i and i + AHEAD < UNITS:
+                load_round(i + AHEAD)
+            if 0 <= i < UNITS:
+                quantise_unit(i)
+            if 0 <= b < B_TILES:
+                gates(b)
+                mix(b)

@@ -24,7 +24,7 @@ UNITS = CHUNKS * B_TILES
 UNIT_COLS = CHUNK * K_PASS
 N_OUT = 2 * MEM
 
-ROW_ORDER_CHUNKS = 1
+ROW_ORDER_CHUNKS = CHUNKS
 W_LEAD = 3
 AHEAD = 6
 C_BUFS = AHEAD

@@ -15,21 +15,26 @@ ACT = mybir.ActivationFunctionType
 BATCH, IN_DIM, MEM = 512, 16128, 256
 K = MEM + IN_DIM
 P = 128
-K_PASS = 4 * P
+PACK = 4
+K_PASS = P * PACK
 PASSES = K // K_PASS
-CHUNK = 4
-CHUNKS = PASSES // CHUNK
 B_TILES = BATCH // P
-UNITS = CHUNKS * B_TILES
-UNIT_COLS = CHUNK * K_PASS
 N_OUT = 2 * MEM
+BANK_WORDS = 512
 
-ROW_ORDER_CHUNKS = CHUNKS
+CHUNK = 4
+UNIT_COLS = CHUNK * K_PASS
+UNITS = (PASSES // CHUNK) * B_TILES
+TRANSPOSES_PER_BANK = BANK_WORDS // P
+BANKS_PER_UNIT = 2 * CHUNK // TRANSPOSES_PER_BANK
+
 W_LEAD = 3
 AHEAD = 6
 C_BUFS = AHEAD
 W_BUFS = (AHEAD + 2) // 2
+STAGE_BUFS = 3
 V_COLS = 160
+RUN = 4
 
 MIN_TS, MAX_TS, EPS = 0.1, 10.0, 1e-6
 SPAN = MAX_TS - MIN_TS
@@ -38,6 +43,8 @@ DECAY_HI = DECAY_LO + SPAN
 INV_HI = 1.0 / DECAY_HI
 INV_SPAN = SPAN / (DECAY_LO * DECAY_HI)
 SHIFT = math.log(DECAY_HI / DECAY_LO)
+H_SQ_FLOOR = 1e-12
+M_SQ_FLOOR = 1e-24
 
 FLOPS = 2 * BATCH * K * N_OUT
 
@@ -47,97 +54,92 @@ def tile_liquidmemorycell_pb_k_kernel(tc, x, h, h_candidate, Wd, bd, Wu, bu, out
     weights = (Wd, Wu)
     with ExitStack() as ctx:
         consts = ctx.enter_context(tc.tile_pool(name="consts", bufs=1))
-        c_pool = ctx.enter_context(tc.tile_pool(name="c_raw", bufs=C_BUFS))
-        w_pool = ctx.enter_context(tc.tile_pool(name="w_raw", bufs=W_BUFS))
-        grouped = ctx.enter_context(tc.tile_pool(name="grouped", bufs=3))
+        c_pool = ctx.enter_context(tc.tile_pool(name="c_rows", bufs=C_BUFS))
+        w_pool = ctx.enter_context(tc.tile_pool(name="w_rows", bufs=W_BUFS))
+        grouped = ctx.enter_context(tc.tile_pool(name="grouped", bufs=STAGE_BUFS))
         w_mx = ctx.enter_context(tc.tile_pool(name="w_mx", bufs=W_LEAD + CHUNK + 1))
-        c_mx = ctx.enter_context(tc.tile_pool(name="c_mx", bufs=3))
-        tail = ctx.enter_context(tc.tile_pool(name="tail", bufs=3))
-        acc_pool = ctx.enter_context(tc.psum_pool(name="acc", bufs=1))
-        xt_pool = ctx.enter_context(tc.psum_pool(name="xt", bufs=4))
+        c_mx = ctx.enter_context(tc.tile_pool(name="c_mx", bufs=STAGE_BUFS))
+        tail = ctx.enter_context(tc.tile_pool(name="tail", bufs=STAGE_BUFS))
+        sums_pool = ctx.enter_context(tc.psum_pool(name="sums", bufs=1))
+        planes_pool = ctx.enter_context(tc.psum_pool(name="planes", bufs=2 * BANKS_PER_UNIT))
         ctx.enter_context(tc.manual_schedule())
 
-        c_raw, w_raw, w_grouped, w_codes, w_scales = {}, {}, {}, {}, {}
-        c_banks, c_grouped, c_codes, c_scales = {}, {}, {}, {}
-        gate, blend, ratios = {}, {}, {}
+        c_rows, c_planes, c_grouped, c_codes, c_scales = {}, {}, {}, {}, {}
+        w_rows, w_grouped, w_codes, w_scales = {}, {}, {}, {}
+        gates, blends, ratios = {}, {}, {}
 
         def load_unit(n):
-            ci, b = divmod(n, B_TILES)
-            rows = slice(b * P, (b + 1) * P)
-            raw = c_pool.tile([P, UNIT_COLS], BF16, name="c_raw")
-            if ci == 0:
-                nc.sync.dma_start(out=raw[:, 0:MEM], in_=h[rows, :])
-                nc.sync.dma_start(out=raw[:, MEM:], in_=x[rows, 0 : UNIT_COLS - MEM])
+            chunk, b = divmod(n, B_TILES)
+            batch_rows = slice(b * P, (b + 1) * P)
+            rows = c_pool.tile([P, UNIT_COLS], BF16, name="c_rows")
+            if chunk == 0:
+                nc.sync.dma_start(out=rows[:, 0:MEM], in_=h[batch_rows, :])
+                nc.sync.dma_start(out=rows[:, MEM:], in_=x[batch_rows, 0 : UNIT_COLS - MEM])
             else:
-                first = ci * UNIT_COLS - MEM
-                nc.sync.dma_start(out=raw[:], in_=x[rows, first : first + UNIT_COLS])
-            c_raw[n] = raw
+                first = chunk * UNIT_COLS - MEM
+                nc.sync.dma_start(out=rows[:], in_=x[batch_rows, first : first + UNIT_COLS])
+            c_rows[n] = rows
 
         def load_weight_pair(q):
-            rows = slice(2 * q * K_PASS, (2 * q + 2) * K_PASS)
-            raw = w_pool.tile([P, 2, 2, 4, MEM], BF16, name="w_raw")
+            k_rows = slice(2 * q * K_PASS, (2 * q + 2) * K_PASS)
+            rows = w_pool.tile([P, 2, 2, PACK, MEM], BF16, name="w_rows")
             for w in range(2):
-                if (2 * q) // CHUNK < ROW_ORDER_CHUNKS:
-                    nc.sync.dma_start(
-                        out=raw[:, w].rearrange("p g t n -> p g (t n)"),
-                        in_=weights[w][rows, :].rearrange("(g p t) n -> p g (t n)", g=2, t=4),
-                    )
-                else:
-                    nc.sync.dma_start(
-                        out=raw[:, w].rearrange("p g (u e) n -> p (g u) (e n)", e=2),
-                        in_=weights[w][rows, :].rearrange("(s p e) n -> p s (e n)", s=4, e=2),
-                    )
-            w_raw[q] = raw
+                nc.sync.dma_start(
+                    out=rows[:, w].rearrange("p g t n -> p g (t n)"),
+                    in_=weights[w][k_rows, :].rearrange("(g p t) n -> p g (t n)", g=2, t=PACK),
+                )
+            w_rows[q] = rows
 
-        def regroup_weights(pn):
-            raw = w_raw[pn // 2]
-            g = pn % 2
-            gw = grouped.tile([P, 2, MEM, 4], BF16, name="gw", align_bytes=64)
+        def load_round(j):
+            load_unit(j)
+            if (j + W_LEAD) % 2 == 0 and j + W_LEAD < PASSES:
+                load_weight_pair((j + W_LEAD) // 2)
+
+        def regroup_weights(g):
+            rows = w_rows[g // 2]
+            side = grouped.tile([P, 2, MEM, PACK], BF16, name="w_grouped", align_bytes=64)
             nc.vector.tensor_copy(
-                out=gw[:, :, 0:V_COLS, :].rearrange("p w (c i) t -> p w c t i", i=4),
-                in_=raw[:, :, g, :, 0:V_COLS].rearrange("p w t (c i) -> p w c t i", i=4),
+                out=side[:, :, 0:V_COLS, :].rearrange("p w (c i) t -> p w c t i", i=RUN),
+                in_=rows[:, :, g % 2, :, 0:V_COLS].rearrange("p w t (c i) -> p w c t i", i=RUN),
             )
             for w in range(2):
                 nc.scalar.copy(
-                    out=gw[:, w, V_COLS:, :].rearrange("p (c i) t -> p c t i", i=4),
-                    in_=raw[:, w, g, :, V_COLS:].rearrange("p t (c i) -> p c t i", i=4),
+                    out=side[:, w, V_COLS:, :].rearrange("p (c i) t -> p c t i", i=RUN),
+                    in_=rows[:, w, g % 2, :, V_COLS:].rearrange("p t (c i) -> p c t i", i=RUN),
                 )
-            w_grouped[pn] = gw
+            w_grouped[g] = side
 
-        def quantise_weights(pn):
+        def quantise_weights(g):
             codes = w_mx.tile([P, N_OUT], U32, name="w_codes", align_bytes=64)
             scales = w_mx.tile([P, N_OUT], U8, name="w_scales", align_bytes=64)
             nc.vector.quantize_mx(
                 out=codes[:].bitcast(FP8X4),
                 scales=scales[:],
-                in_=w_grouped[pn][:].rearrange("p w n t -> p (w n t)"),
+                in_=w_grouped[g][:].rearrange("p w n t -> p (w n t)"),
             )
-            w_codes[pn], w_scales[pn] = codes, scales
+            w_codes[g], w_scales[g] = codes, scales
 
         def transpose_unit(n):
-            ci = n // B_TILES
-            words = c_raw[n][:].bitcast(F32)
-            if ci < ROW_ORDER_CHUNKS:
-                planes = words.rearrange("r (g p u) -> r g u p", g=CHUNK, u=2)
-            else:
-                planes = words.rearrange("r (g u p) -> r g u p", g=CHUNK, u=2)
+            words = c_rows[n][:].bitcast(F32)
+            planes = words.rearrange("r (g p u) -> r g u p", g=CHUNK, u=2)
             banks = []
-            for half in range(2):
-                xt = xt_pool.tile([P, 4, P], F32, name="xt")
-                for j in range(4):
-                    nc.tensor.transpose(xt[:, j, :], planes[:, 2 * half + j // 2, j % 2, :], ident[:])
-                banks.append(xt)
-            c_banks[n] = banks
+            for f in range(BANKS_PER_UNIT):
+                bank = planes_pool.tile([P, TRANSPOSES_PER_BANK, P], F32, name="planes")
+                for j in range(TRANSPOSES_PER_BANK):
+                    g, u = divmod(f * TRANSPOSES_PER_BANK + j, 2)
+                    nc.tensor.transpose(bank[:, j, :], planes[:, g, u, :], identity[:])
+                banks.append(bank)
+            c_planes[n] = banks
 
         def copy_out_unit(n):
-            gx = grouped.tile([P, UNIT_COLS], BF16, name="gx", align_bytes=64)
-            gx_words = gx[:].bitcast(F32).rearrange("p (f g r u) -> p f g r u", f=2, g=2, u=2)
-            for half in range(2):
+            side = grouped.tile([P, UNIT_COLS], BF16, name="c_grouped", align_bytes=64)
+            side_words = side[:].bitcast(F32).rearrange("p (f g r u) -> p f g r u", f=BANKS_PER_UNIT, r=P, u=2)
+            for f in range(BANKS_PER_UNIT):
                 nc.scalar.copy(
-                    out=gx_words[:, half],
-                    in_=c_banks[n][half][:].rearrange("p (g u) r -> p g r u", u=2),
+                    out=side_words[:, f],
+                    in_=c_planes[n][f][:].rearrange("p (g u) r -> p g r u", u=2),
                 )
-            c_grouped[n] = gx
+            c_grouped[n] = side
 
         def quantise_unit(n):
             codes = c_mx.tile([P, CHUNK * P], U32, name="c_codes", align_bytes=64)
@@ -146,68 +148,67 @@ def tile_liquidmemorycell_pb_k_kernel(tc, x, h, h_candidate, Wd, bd, Wu, bu, out
             c_codes[n], c_scales[n] = codes, scales
 
         def multiply_unit(n):
-            ci, b = divmod(n, B_TILES)
-            for g in range(CHUNK):
-                pn = ci * CHUNK + g
-                rows = slice(g * P, (g + 1) * P)
+            chunk, b = divmod(n, B_TILES)
+            for j in range(CHUNK):
+                g = chunk * CHUNK + j
+                cols = slice(j * P, (j + 1) * P)
                 nc.tensor.matmul_mx(
-                    out=acc[b][:],
-                    lhsT=c_codes[n][:, rows].bitcast(FP8X4),
-                    lhsT_scale=c_scales[n][:, rows],
-                    rhs=w_codes[pn][:].bitcast(FP8X4),
-                    rhs_scale=w_scales[pn][:],
-                    start=(pn == 0),
-                    stop=(pn == PASSES - 1),
+                    out=sums[b][:],
+                    lhsT=c_codes[n][:, cols].bitcast(FP8X4),
+                    lhsT_scale=c_scales[n][:, cols],
+                    rhs=w_codes[g][:].bitcast(FP8X4),
+                    rhs_scale=w_scales[g][:],
+                    start=(g == 0),
+                    stop=(g == PASSES - 1),
                 )
 
-        def prepare_from_h(b):
-            h_cols = c_raw[b][:, 0:MEM]
-            square = tail.tile([P, MEM], F32, name="square")
+        def keep_h(b):
+            h_cols = c_rows[b][:, 0:MEM]
+            squares = tail.tile([P, MEM], F32, name="squares")
             nc.scalar.activation(out=h_span[:, b, :], in_=h_cols, func=ACT.Copy, scale=INV_SPAN)
-            nc.scalar.activation(out=square[:], in_=h_cols, func=ACT.Square, accum_out=h_sq[:, b : b + 1])
+            nc.scalar.activation(out=squares[:], in_=h_cols, func=ACT.Square, accum_out=h_sq[:, b : b + 1])
+
+        def prepare_epilogue():
+            nc.gpsimd.tensor_scalar(out=h_norm[:], in0=h_sq[:], scalar1=H_SQ_FLOOR, scalar2=None, op0=ALU.max)
+            nc.gpsimd.tensor_tensor(out=h_norm[:], in0=h_norm[:], in1=plus_half[:], op=ALU.pow)
             nc.vector.scalar_tensor_tensor(
-                out=rest[:, b, :], in0=h_cols, scalar=INV_HI, in1=cand[:, b, :], op0=ALU.mult, op1=ALU.subtract
+                out=rest[:], in0=h_span[:], scalar=INV_HI / INV_SPAN, in1=candidate[:], op0=ALU.mult, op1=ALU.subtract
             )
 
-        def gates(b):
-            z = tail.tile([P, N_OUT], F32, name="z")
-            s = tail.tile([P, N_OUT], F32, name="s")
+        def open_gates(b):
+            biased = tail.tile([P, N_OUT], F32, name="biased")
+            gate = tail.tile([P, N_OUT], F32, name="gate")
             for cols in (slice(0, MEM), slice(MEM, N_OUT)):
-                nc.vector.tensor_tensor(out=z[:, cols], in0=acc[b][:, cols], in1=bias_all[:, cols], op=ALU.add)
-                nc.scalar.activation(out=s[:, cols], in_=z[:, cols], func=ACT.Sigmoid, scale=-1.0)
-            gate[b] = s
+                nc.vector.tensor_tensor(out=biased[:, cols], in0=sums[b][:, cols], in1=bias_all[:, cols], op=ALU.add)
+                nc.scalar.activation(out=gate[:, cols], in_=biased[:, cols], func=ACT.Sigmoid, scale=-1.0)
+            gates[b] = gate
 
-        def mix(b):
-            s = gate[b]
+        def blend(b):
+            gate = gates[b]
             m = tail.tile([P, MEM], F32, name="m")
-            nc.vector.tensor_tensor(out=m[:], in0=s[:, 0:MEM], in1=h_span[:, b, :], op=ALU.mult)
+            nc.vector.tensor_tensor(out=m[:], in0=gate[:, 0:MEM], in1=h_span[:, b, :], op=ALU.mult)
             nc.vector.tensor_tensor(out=m[:], in0=m[:], in1=rest[:, b, :], op=ALU.add)
-            nc.vector.tensor_tensor(out=m[:], in0=m[:], in1=s[:, MEM:], op=ALU.mult)
-            nc.vector.tensor_tensor(out=m[:], in0=m[:], in1=cand[:, b, :], op=ALU.add)
-            blend[b] = m
+            nc.vector.tensor_tensor(out=m[:], in0=m[:], in1=gate[:, MEM:], op=ALU.mult)
+            nc.vector.tensor_tensor(out=m[:], in0=m[:], in1=candidate[:, b, :], op=ALU.add)
+            blends[b] = m
 
         def norm_ratio(b):
-            square = tail.tile([P, MEM], F32, name="square")
+            squares = tail.tile([P, MEM], F32, name="squares")
             m_sq = tail.tile([P, 1], F32, name="m_sq")
-            nc.scalar.activation(out=square[:], in_=blend[b][:], func=ACT.Square, accum_out=m_sq[:])
+            nc.scalar.activation(out=squares[:], in_=blends[b][:], func=ACT.Square, accum_out=m_sq[:])
             ratio = tail.tile([P, 1], F32, name="ratio")
-            nc.gpsimd.tensor_scalar(out=ratio[:], in0=m_sq[:], scalar1=1e-24, scalar2=None, op0=ALU.max)
+            nc.gpsimd.tensor_scalar(out=ratio[:], in0=m_sq[:], scalar1=M_SQ_FLOOR, scalar2=None, op0=ALU.max)
             nc.gpsimd.tensor_tensor(out=ratio[:], in0=ratio[:], in1=minus_half[:], op=ALU.pow)
             nc.gpsimd.tensor_tensor(out=ratio[:], in0=ratio[:], in1=h_norm[:, b : b + 1], op=ALU.mult)
             ratios[b] = ratio
 
         def store_tile(b):
             result = tail.tile([P, MEM], F32, name="result")
-            nc.scalar.activation(out=result[:], in_=blend[b][:], func=ACT.Copy, scale=ratios[b][:])
+            nc.scalar.activation(out=result[:], in_=blends[b][:], func=ACT.Copy, scale=ratios[b][:])
             nc.sync.dma_start(out=out[b * P : (b + 1) * P, :], in_=result[:])
 
-        def load_round(j):
-            if (j + W_LEAD) % 2 == 0 and j + W_LEAD < PASSES:
-                load_weight_pair((j + W_LEAD) // 2)
-            load_unit(j)
-
-        ident = consts.tile([P, P], F32, name="ident")
-        make_identity(nc, ident[:])
+        identity = consts.tile([P, P], F32, name="identity")
+        make_identity(nc, identity[:])
         plus_half = consts.tile([P, B_TILES], F32, name="plus_half")
         nc.gpsimd.memset(plus_half[:], 0.5)
         minus_half = consts.tile([P, 1], F32, name="minus_half")
@@ -225,12 +226,12 @@ def tile_liquidmemorycell_pb_k_kernel(tc, x, h, h_candidate, Wd, bd, Wu, bu, out
         nc.sync.dma_start(out=bias_row[0:1, MEM:], in_=bu.rearrange("(o n) -> o n", o=1))
         for q in range((W_LEAD + 1) // 2):
             load_weight_pair(q)
-        cand = consts.tile([P, B_TILES, MEM], BF16, name="cand")
-        nc.sync.dma_start(out=cand[:], in_=h_candidate.rearrange("(b p) n -> p b n", p=P))
         for j in range(AHEAD):
             load_round(j)
+        candidate = consts.tile([P, B_TILES, MEM], BF16, name="candidate")
+        nc.sync.dma_start(out=candidate[:], in_=h_candidate.rearrange("(b p) n -> p b n", p=P))
 
-        bias_bank = xt_pool.tile([P, N_OUT], F32, name="xt")
+        bias_bank = planes_pool.tile([P, N_OUT], F32, name="planes")
         nc.tensor.matmul(out=bias_bank[:], lhsT=ones[:], rhs=bias_row[:], start=True, stop=True)
         bias_all = consts.tile([P, N_OUT], F32, name="bias_all")
         nc.vector.tensor_scalar_add(out=bias_all[:, 0:MEM], in0=bias_bank[:, 0:MEM], scalar1=SHIFT)
@@ -240,16 +241,16 @@ def tile_liquidmemorycell_pb_k_kernel(tc, x, h, h_candidate, Wd, bd, Wu, bu, out
         rest = consts.tile([P, B_TILES, MEM], F32, name="rest")
         h_sq = consts.tile([P, B_TILES], F32, name="h_sq")
         h_norm = consts.tile([P, B_TILES], F32, name="h_norm")
-        acc = []
+        sums = []
         for b in range(B_TILES):
-            bank = acc_pool.tile([P, N_OUT], F32, name="acc%d" % b)
-            acc.append(bank)
+            bank = sums_pool.tile([P, N_OUT], F32, name="sums%d" % b)
+            sums.append(bank)
 
         for i in range(-W_LEAD, UNITS + 3):
-            pn = i + W_LEAD
+            g = i + W_LEAD
             b = i - 1 - (UNITS - B_TILES)
-            if 1 <= pn <= PASSES:
-                quantise_weights(pn - 1)
+            if 1 <= g <= PASSES:
+                quantise_weights(g - 1)
             if 0 <= i < UNITS:
                 transpose_unit(i)
             if 1 <= i <= UNITS:
@@ -257,20 +258,19 @@ def tile_liquidmemorycell_pb_k_kernel(tc, x, h, h_candidate, Wd, bd, Wu, bu, out
             if 0 <= i < UNITS:
                 copy_out_unit(i)
             if 0 <= i < B_TILES:
-                prepare_from_h(i)
-            if i == B_TILES:
-                nc.gpsimd.tensor_scalar(out=h_norm[:], in0=h_sq[:], scalar1=1e-12, scalar2=None, op0=ALU.max)
-                nc.gpsimd.tensor_tensor(out=h_norm[:], in0=h_norm[:], in1=plus_half[:], op=ALU.pow)
+                keep_h(i)
             if 0 <= b - 2 < B_TILES:
                 store_tile(b - 2)
             if 0 <= b - 1 < B_TILES:
                 norm_ratio(b - 1)
-            if pn < PASSES:
-                regroup_weights(pn)
+            if g < PASSES:
+                regroup_weights(g)
             if 0 <= i and i + AHEAD < UNITS:
                 load_round(i + AHEAD)
             if 0 <= i < UNITS:
                 quantise_unit(i)
+            if i == AHEAD:
+                prepare_epilogue()
             if 0 <= b < B_TILES:
-                gates(b)
-                mix(b)
+                open_gates(b)
+                blend(b)

@@ -59,14 +59,14 @@ def tile_liquidmemorycell_pb_k_kernel(tc, x, h, h_candidate, Wd, bd, Wu, bu, out
         grouped = ctx.enter_context(tc.tile_pool(name="grouped", bufs=STAGE_BUFS))
         w_mx = ctx.enter_context(tc.tile_pool(name="w_mx", bufs=W_LEAD + CHUNK + 1))
         c_mx = ctx.enter_context(tc.tile_pool(name="c_mx", bufs=STAGE_BUFS))
-        tail = ctx.enter_context(tc.tile_pool(name="tail", bufs=STAGE_BUFS))
+        tail = ctx.enter_context(tc.tile_pool(name="tail", bufs=4))
         sums_pool = ctx.enter_context(tc.psum_pool(name="sums", bufs=1))
         planes_pool = ctx.enter_context(tc.psum_pool(name="planes", bufs=2 * BANKS_PER_UNIT))
         ctx.enter_context(tc.manual_schedule())
 
         c_rows, c_planes, c_grouped, c_codes, c_scales = {}, {}, {}, {}, {}
         w_rows, w_grouped, w_codes, w_scales = {}, {}, {}, {}
-        gates, blends, ratios = {}, {}, {}
+        biased, gates, blends, ratios = {}, {}, {}, {}
 
         def load_unit(n):
             chunk, b = divmod(n, B_TILES)
@@ -175,22 +175,26 @@ def tile_liquidmemorycell_pb_k_kernel(tc, x, h, h_candidate, Wd, bd, Wu, bu, out
                 out=rest[:], in0=h_span[:], scalar=INV_HI / INV_SPAN, in1=candidate[:], op0=ALU.mult, op1=ALU.subtract
             )
 
-        def open_gates(b):
-            biased = tail.tile([P, N_OUT], F32, name="biased")
-            gate = tail.tile([P, N_OUT], F32, name="gate")
-            for cols in (slice(0, MEM), slice(MEM, N_OUT)):
-                nc.vector.tensor_tensor(out=biased[:, cols], in0=sums[b][:, cols], in1=bias_all[:, cols], op=ALU.add)
-                nc.scalar.activation(out=gate[:, cols], in_=biased[:, cols], func=ACT.Sigmoid, scale=-1.0)
-            gates[b] = gate
+        def add_bias(b, k):
+            if k == 0:
+                biased[b] = tail.tile([P, N_OUT], F32, name="biased")
+            cols = slice(k * MEM, (k + 1) * MEM)
+            nc.vector.tensor_tensor(out=biased[b][:, cols], in0=sums[b][:, cols], in1=bias_all[:, cols], op=ALU.add)
 
-        def blend(b):
+        def sigmoid(b, k):
+            if k == 0:
+                gates[b] = tail.tile([P, N_OUT], F32, name="gate")
+            cols = slice(k * MEM, (k + 1) * MEM)
+            nc.scalar.activation(out=gates[b][:, cols], in_=biased[b][:, cols], func=ACT.Sigmoid, scale=-1.0)
+
+        def blend_step(b, k):
             gate = gates[b]
-            m = tail.tile([P, MEM], F32, name="m")
-            nc.vector.tensor_tensor(out=m[:], in0=gate[:, 0:MEM], in1=h_span[:, b, :], op=ALU.mult)
-            nc.vector.tensor_tensor(out=m[:], in0=m[:], in1=rest[:, b, :], op=ALU.add)
-            nc.vector.tensor_tensor(out=m[:], in0=m[:], in1=gate[:, MEM:], op=ALU.mult)
-            nc.vector.tensor_tensor(out=m[:], in0=m[:], in1=candidate[:, b, :], op=ALU.add)
-            blends[b] = m
+            if k == 0:
+                blends[b] = tail.tile([P, MEM], F32, name="m")
+            m = blends[b]
+            in0 = (gate[:, 0:MEM], m[:], m[:], m[:])[k]
+            in1 = (h_span[:, b, :], rest[:, b, :], gate[:, MEM:], candidate[:, b, :])[k]
+            nc.vector.tensor_tensor(out=m[:], in0=in0, in1=in1, op=(ALU.mult, ALU.add, ALU.mult, ALU.add)[k])
 
         def norm_ratio(b):
             squares = tail.tile([P, MEM], F32, name="squares")
@@ -246,7 +250,7 @@ def tile_liquidmemorycell_pb_k_kernel(tc, x, h, h_candidate, Wd, bd, Wu, bu, out
             bank = sums_pool.tile([P, N_OUT], F32, name="sums%d" % b)
             sums.append(bank)
 
-        for i in range(-W_LEAD, UNITS + 3):
+        for i in range(-W_LEAD, UNITS + 4):
             g = i + W_LEAD
             b = i - 1 - (UNITS - B_TILES)
             if 1 <= g <= PASSES:
@@ -259,18 +263,31 @@ def tile_liquidmemorycell_pb_k_kernel(tc, x, h, h_candidate, Wd, bd, Wu, bu, out
                 copy_out_unit(i)
             if 0 <= i < B_TILES:
                 keep_h(i)
-            if 0 <= b - 2 < B_TILES:
-                store_tile(b - 2)
             if 0 <= b - 1 < B_TILES:
-                norm_ratio(b - 1)
+                sigmoid(b - 1, 0)
+            if 0 <= b - 1 < B_TILES:
+                sigmoid(b - 1, 1)
+            if 0 <= b - 3 < B_TILES:
+                store_tile(b - 3)
+            if 0 <= b - 2 < B_TILES:
+                norm_ratio(b - 2)
             if g < PASSES:
                 regroup_weights(g)
             if 0 <= i and i + AHEAD < UNITS:
                 load_round(i + AHEAD)
+            if i == AHEAD + 1:
+                prepare_epilogue()
+            if 0 <= b - 1 < B_TILES:
+                blend_step(b - 1, 0)
             if 0 <= i < UNITS:
                 quantise_unit(i)
-            if i == AHEAD:
-                prepare_epilogue()
-            if 0 <= b < B_TILES:
-                open_gates(b)
-                blend(b)
+            if 0 <= b - 1 < B_TILES:
+                blend_step(b - 1, 1)
+            if 0 <= b - 0 < B_TILES:
+                add_bias(b - 0, 0)
+            if 0 <= b - 1 < B_TILES:
+                blend_step(b - 1, 2)
+            if 0 <= b - 0 < B_TILES:
+                add_bias(b - 0, 1)
+            if 0 <= b - 1 < B_TILES:
+                blend_step(b - 1, 3)

@@ -42,6 +42,7 @@ DECAY_LO = MIN_TS + EPS
 DECAY_HI = DECAY_LO + SPAN
 INV_HI = 1.0 / DECAY_HI
 INV_SPAN = SPAN / (DECAY_LO * DECAY_HI)
+S_ADD = INV_HI / INV_SPAN
 SHIFT = math.log(DECAY_HI / DECAY_LO)
 H_SQ_FLOOR = 1e-12
 M_SQ_FLOOR = 1e-24
@@ -169,11 +170,8 @@ def tile_liquidmemorycell_pb_k_kernel(tc, x, h, h_candidate, Wd, bd, Wu, bu, out
             nc.scalar.activation(out=squares[:], in_=h_cols, func=ACT.Square, accum_out=h_sq[:, b : b + 1])
 
         def prepare_epilogue():
-            nc.gpsimd.tensor_scalar(out=h_norm[:], in0=h_sq[:], scalar1=H_SQ_FLOOR, scalar2=None, op0=ALU.max)
-            nc.gpsimd.tensor_tensor(out=h_norm[:], in0=h_norm[:], in1=plus_half[:], op=ALU.pow)
-            nc.vector.scalar_tensor_tensor(
-                out=rest[:], in0=h_span[:], scalar=INV_HI / INV_SPAN, in1=candidate[:], op0=ALU.mult, op1=ALU.subtract
-            )
+            nc.gpsimd.tensor_scalar(out=inv_h_sq[:], in0=h_sq[:], scalar1=H_SQ_FLOOR, scalar2=None, op0=ALU.max)
+            nc.gpsimd.tensor_tensor(out=inv_h_sq[:], in0=inv_h_sq[:], in1=minus_one[:], op=ALU.pow)
 
         def add_bias(b, k):
             if k == 0:
@@ -187,23 +185,31 @@ def tile_liquidmemorycell_pb_k_kernel(tc, x, h, h_candidate, Wd, bd, Wu, bu, out
             cols = slice(k * MEM, (k + 1) * MEM)
             nc.scalar.activation(out=gates[b][:, cols], in_=biased[b][:, cols], func=ACT.Sigmoid, scale=-1.0)
 
-        def blend_step(b, k):
+        def blend_step(b, step):
             gate = gates[b]
-            if k == 0:
+            if step == 0:
                 blends[b] = tail.tile([P, MEM], F32, name="m")
             m = blends[b]
-            in0 = (gate[:, 0:MEM], m[:], m[:], m[:])[k]
-            in1 = (h_span[:, b, :], rest[:, b, :], gate[:, MEM:], candidate[:, b, :])[k]
-            nc.vector.tensor_tensor(out=m[:], in0=in0, in1=in1, op=(ALU.mult, ALU.add, ALU.mult, ALU.add)[k])
+            if step == 0:
+                nc.vector.scalar_tensor_tensor(
+                    out=m[:], in0=gate[:, 0:MEM], scalar=S_ADD, in1=h_span[:, b, :], op0=ALU.add, op1=ALU.mult
+                )
+            elif step == 1:
+                nc.vector.tensor_tensor(out=m[:], in0=m[:], in1=candidate[:, b, :], op=ALU.subtract)
+            elif step == 2:
+                nc.vector.tensor_tensor(out=m[:], in0=m[:], in1=gate[:, MEM:], op=ALU.mult)
+            else:
+                nc.vector.tensor_tensor(out=m[:], in0=m[:], in1=candidate[:, b, :], op=ALU.add)
 
         def norm_ratio(b):
             squares = tail.tile([P, MEM], F32, name="squares")
             m_sq = tail.tile([P, 1], F32, name="m_sq")
             nc.scalar.activation(out=squares[:], in_=blends[b][:], func=ACT.Square, accum_out=m_sq[:])
             ratio = tail.tile([P, 1], F32, name="ratio")
-            nc.gpsimd.tensor_scalar(out=ratio[:], in0=m_sq[:], scalar1=M_SQ_FLOOR, scalar2=None, op0=ALU.max)
+            nc.gpsimd.tensor_scalar(
+                out=ratio[:], in0=m_sq[:], scalar1=M_SQ_FLOOR, scalar2=inv_h_sq[:, b : b + 1], op0=ALU.max, op1=ALU.mult
+            )
             nc.gpsimd.tensor_tensor(out=ratio[:], in0=ratio[:], in1=minus_half[:], op=ALU.pow)
-            nc.gpsimd.tensor_tensor(out=ratio[:], in0=ratio[:], in1=h_norm[:, b : b + 1], op=ALU.mult)
             ratios[b] = ratio
 
         def store_tile(b):
@@ -213,8 +219,8 @@ def tile_liquidmemorycell_pb_k_kernel(tc, x, h, h_candidate, Wd, bd, Wu, bu, out
 
         identity = consts.tile([P, P], F32, name="identity")
         make_identity(nc, identity[:])
-        plus_half = consts.tile([P, B_TILES], F32, name="plus_half")
-        nc.gpsimd.memset(plus_half[:], 0.5)
+        minus_one = consts.tile([P, B_TILES], F32, name="minus_one")
+        nc.gpsimd.memset(minus_one[:], -1.0)
         minus_half = consts.tile([P, 1], F32, name="minus_half")
         nc.gpsimd.memset(minus_half[:], -0.5)
 
@@ -233,7 +239,6 @@ def tile_liquidmemorycell_pb_k_kernel(tc, x, h, h_candidate, Wd, bd, Wu, bu, out
         for j in range(AHEAD):
             load_round(j)
         candidate = consts.tile([P, B_TILES, MEM], BF16, name="candidate")
-        nc.sync.dma_start(out=candidate[:], in_=h_candidate.rearrange("(b p) n -> p b n", p=P))
 
         bias_bank = planes_pool.tile([P, N_OUT], F32, name="planes")
         nc.tensor.matmul(out=bias_bank[:], lhsT=ones[:], rhs=bias_row[:], start=True, stop=True)
@@ -242,9 +247,8 @@ def tile_liquidmemorycell_pb_k_kernel(tc, x, h, h_candidate, Wd, bd, Wu, bu, out
         nc.vector.tensor_copy(out=bias_all[:, MEM:], in_=bias_bank[:, MEM:])
 
         h_span = consts.tile([P, B_TILES, MEM], F32, name="h_span")
-        rest = consts.tile([P, B_TILES, MEM], F32, name="rest")
         h_sq = consts.tile([P, B_TILES], F32, name="h_sq")
-        h_norm = consts.tile([P, B_TILES], F32, name="h_norm")
+        inv_h_sq = consts.tile([P, B_TILES], F32, name="inv_h_sq")
         sums = []
         for b in range(B_TILES):
             bank = sums_pool.tile([P, N_OUT], F32, name="sums%d" % b)
@@ -275,7 +279,9 @@ def tile_liquidmemorycell_pb_k_kernel(tc, x, h, h_candidate, Wd, bd, Wu, bu, out
                 regroup_weights(g)
             if 0 <= i and i + AHEAD < UNITS:
                 load_round(i + AHEAD)
-            if i == AHEAD + 1:
+            if i + AHEAD == UNITS:
+                nc.sync.dma_start(out=candidate[:], in_=h_candidate.rearrange("(b p) n -> p b n", p=P))
+            if i == B_TILES:
                 prepare_epilogue()
             if 0 <= b - 1 < B_TILES:
                 blend_step(b - 1, 0)

@@ -53,6 +53,8 @@ FLOPS = 2 * BATCH * K * N_OUT
 def tile_liquidmemorycell_pb_k_kernel(tc, x, h, h_candidate, Wd, bd, Wu, bu, out):
     nc = tc.nc
     weights = (Wd, Wu)
+    x_tiles = x.rearrange("(p b) k -> p b k", b=B_TILES)
+    out_tiles = out.rearrange("(p b) n -> p b n", b=B_TILES)
     with ExitStack() as ctx:
         consts = ctx.enter_context(tc.tile_pool(name="consts", bufs=1))
         c_pool = ctx.enter_context(tc.tile_pool(name="c_rows", bufs=C_BUFS))
@@ -71,14 +73,12 @@ def tile_liquidmemorycell_pb_k_kernel(tc, x, h, h_candidate, Wd, bd, Wu, bu, out
 
         def load_unit(n):
             chunk, b = divmod(n, B_TILES)
-            batch_rows = slice(b * P, (b + 1) * P)
             rows = c_pool.tile([P, UNIT_COLS], BF16, name="c_rows")
             if chunk == 0:
-                nc.sync.dma_start(out=rows[:, 0:MEM], in_=h[batch_rows, :])
-                nc.sync.dma_start(out=rows[:, MEM:], in_=x[batch_rows, 0 : UNIT_COLS - MEM])
+                nc.sync.dma_start(out=rows[:, MEM:], in_=x_tiles[:, b, 0 : UNIT_COLS - MEM])
             else:
                 first = chunk * UNIT_COLS - MEM
-                nc.sync.dma_start(out=rows[:], in_=x[batch_rows, first : first + UNIT_COLS])
+                nc.sync.dma_start(out=rows[:], in_=x_tiles[:, b, first : first + UNIT_COLS])
             c_rows[n] = rows
 
         def load_weight_pair(q):
@@ -164,7 +164,7 @@ def tile_liquidmemorycell_pb_k_kernel(tc, x, h, h_candidate, Wd, bd, Wu, bu, out
                 )
 
         def keep_h(b):
-            h_cols = c_rows[b][:, 0:MEM]
+            h_cols = h_rows[:, b, :]
             squares = tail.tile([P, MEM], F32, name="squares")
             nc.scalar.activation(out=h_span[:, b, :], in_=h_cols, func=ACT.Copy, scale=INV_SPAN)
             nc.scalar.activation(out=squares[:], in_=h_cols, func=ACT.Square, accum_out=h_sq[:, b : b + 1])
@@ -172,6 +172,12 @@ def tile_liquidmemorycell_pb_k_kernel(tc, x, h, h_candidate, Wd, bd, Wu, bu, out
         def prepare_epilogue():
             nc.gpsimd.tensor_scalar(out=inv_h_sq[:], in0=h_sq[:], scalar1=H_SQ_FLOOR, scalar2=None, op0=ALU.max)
             nc.gpsimd.tensor_tensor(out=inv_h_sq[:], in0=inv_h_sq[:], in1=minus_one[:], op=ALU.pow)
+
+        def spread_biases():
+            bias_bank = planes_pool.tile([P, N_OUT], F32, name="planes")
+            nc.tensor.matmul(out=bias_bank[:], lhsT=ones[:], rhs=bias_row[:], start=True, stop=True)
+            nc.vector.tensor_scalar_add(out=bias_all[:, 0:MEM], in0=bias_bank[:, 0:MEM], scalar1=SHIFT)
+            nc.vector.tensor_copy(out=bias_all[:, MEM:], in_=bias_bank[:, MEM:])
 
         def add_bias(b, k):
             if k == 0:
@@ -215,7 +221,7 @@ def tile_liquidmemorycell_pb_k_kernel(tc, x, h, h_candidate, Wd, bd, Wu, bu, out
         def store_tile(b):
             result = tail.tile([P, MEM], F32, name="result")
             nc.scalar.activation(out=result[:], in_=blends[b][:], func=ACT.Copy, scale=ratios[b][:])
-            nc.sync.dma_start(out=out[b * P : (b + 1) * P, :], in_=result[:])
+            nc.sync.dma_start(out=out_tiles[:, b, :], in_=result[:])
 
         identity = consts.tile([P, P], F32, name="identity")
         make_identity(nc, identity[:])
@@ -232,19 +238,20 @@ def tile_liquidmemorycell_pb_k_kernel(tc, x, h, h_candidate, Wd, bd, Wu, bu, out
         nc.vector.memset(warm[:], 0.0)
         nc.scalar.activation(out=warm[:], in_=warm[:], func=ACT.Sigmoid)
 
-        nc.sync.dma_start(out=bias_row[0:1, 0:MEM], in_=bd.rearrange("(o n) -> o n", o=1))
-        nc.sync.dma_start(out=bias_row[0:1, MEM:], in_=bu.rearrange("(o n) -> o n", o=1))
-        for q in range((W_LEAD + 1) // 2):
-            load_weight_pair(q)
-        for j in range(AHEAD):
+        h_rows = consts.tile([P, B_TILES, MEM], BF16, name="h_rows")
+        load_weight_pair(0)
+        nc.sync.dma_start(
+            out=h_rows[:].rearrange("p b n -> p (b n)"), in_=h.rearrange("(p b) n -> p (b n)", b=B_TILES)
+        )
+        load_round(0)
+        load_weight_pair(1)
+        for j in range(1, AHEAD):
             load_round(j)
         candidate = consts.tile([P, B_TILES, MEM], BF16, name="candidate")
 
-        bias_bank = planes_pool.tile([P, N_OUT], F32, name="planes")
-        nc.tensor.matmul(out=bias_bank[:], lhsT=ones[:], rhs=bias_row[:], start=True, stop=True)
+        nc.sync.dma_start(out=bias_row[0:1, 0:MEM], in_=bd.rearrange("(o n) -> o n", o=1))
+        nc.sync.dma_start(out=bias_row[0:1, MEM:], in_=bu.rearrange("(o n) -> o n", o=1))
         bias_all = consts.tile([P, N_OUT], F32, name="bias_all")
-        nc.vector.tensor_scalar_add(out=bias_all[:, 0:MEM], in0=bias_bank[:, 0:MEM], scalar1=SHIFT)
-        nc.vector.tensor_copy(out=bias_all[:, MEM:], in_=bias_bank[:, MEM:])
 
         h_span = consts.tile([P, B_TILES, MEM], F32, name="h_span")
         h_sq = consts.tile([P, B_TILES], F32, name="h_sq")
@@ -259,6 +266,9 @@ def tile_liquidmemorycell_pb_k_kernel(tc, x, h, h_candidate, Wd, bd, Wu, bu, out
             b = i - 1 - (UNITS - B_TILES)
             if 1 <= g <= PASSES:
                 quantise_weights(g - 1)
+            if i == -1:
+                for n in range(B_TILES):
+                    nc.scalar.copy(out=c_rows[n][:, 0:MEM], in_=h_rows[:, n, :])
             if 0 <= i < UNITS:
                 transpose_unit(i)
             if 1 <= i <= UNITS:
@@ -280,8 +290,12 @@ def tile_liquidmemorycell_pb_k_kernel(tc, x, h, h_candidate, Wd, bd, Wu, bu, out
             if 0 <= i and i + AHEAD < UNITS:
                 load_round(i + AHEAD)
             if i + AHEAD == UNITS:
-                nc.sync.dma_start(out=candidate[:], in_=h_candidate.rearrange("(b p) n -> p b n", p=P))
-            if i == B_TILES:
+                nc.sync.dma_start(
+                    out=candidate[:].rearrange("p b n -> p (b n)"),
+                    in_=h_candidate.rearrange("(p b) n -> p (b n)", b=B_TILES),
+                )
+            if i == AHEAD:
+                spread_biases()
                 prepare_epilogue()
             if 0 <= b - 1 < B_TILES:
                 blend_step(b - 1, 0)

@@ -176,8 +176,8 @@ def tile_liquidmemorycell_pb_k_kernel(tc, x, h, h_candidate, Wd, bd, Wu, bu, out
         def spread_biases():
             bias_bank = planes_pool.tile([P, N_OUT], F32, name="planes")
             nc.tensor.matmul(out=bias_bank[:], lhsT=ones[:], rhs=bias_row[:], start=True, stop=True)
-            nc.vector.tensor_scalar_add(out=bias_all[:, 0:MEM], in0=bias_bank[:, 0:MEM], scalar1=SHIFT)
-            nc.vector.tensor_copy(out=bias_all[:, MEM:], in_=bias_bank[:, MEM:])
+            nc.scalar.activation(out=bias_all[:, 0:MEM], in_=bias_bank[:, 0:MEM], func=ACT.Identity, bias=SHIFT)
+            nc.scalar.copy(out=bias_all[:, MEM:], in_=bias_bank[:, MEM:])
 
         def add_bias(b, k):
             if k == 0:
@@ -243,14 +243,14 @@ def tile_liquidmemorycell_pb_k_kernel(tc, x, h, h_candidate, Wd, bd, Wu, bu, out
         nc.sync.dma_start(
             out=h_rows[:].rearrange("p b n -> p (b n)"), in_=h.rearrange("(p b) n -> p (b n)", b=B_TILES)
         )
+        nc.sync.dma_start(out=bias_row[0:1, 0:MEM], in_=bd.rearrange("(o n) -> o n", o=1))
+        nc.sync.dma_start(out=bias_row[0:1, MEM:], in_=bu.rearrange("(o n) -> o n", o=1))
         load_round(0)
         load_weight_pair(1)
         for j in range(1, AHEAD):
             load_round(j)
         candidate = consts.tile([P, B_TILES, MEM], BF16, name="candidate")
 
-        nc.sync.dma_start(out=bias_row[0:1, 0:MEM], in_=bd.rearrange("(o n) -> o n", o=1))
-        nc.sync.dma_start(out=bias_row[0:1, MEM:], in_=bu.rearrange("(o n) -> o n", o=1))
         bias_all = consts.tile([P, N_OUT], F32, name="bias_all")
 
         h_span = consts.tile([P, B_TILES, MEM], F32, name="h_span")
@@ -261,7 +261,7 @@ def tile_liquidmemorycell_pb_k_kernel(tc, x, h, h_candidate, Wd, bd, Wu, bu, out
             bank = sums_pool.tile([P, N_OUT], F32, name="sums%d" % b)
             sums.append(bank)
 
-        for i in range(-W_LEAD, UNITS + 4):
+        for i in range(-W_LEAD, UNITS + 5):
             g = i + W_LEAD
             b = i - 1 - (UNITS - B_TILES)
             if 1 <= g <= PASSES:
@@ -269,16 +269,15 @@ def tile_liquidmemorycell_pb_k_kernel(tc, x, h, h_candidate, Wd, bd, Wu, bu, out
             if i == -1:
                 for n in range(B_TILES):
                     nc.scalar.copy(out=c_rows[n][:, 0:MEM], in_=h_rows[:, n, :])
+                spread_biases()
             if 0 <= i < UNITS:
                 transpose_unit(i)
             if 1 <= i <= UNITS:
                 multiply_unit(i - 1)
             if 0 <= i < UNITS:
                 copy_out_unit(i)
-            if 0 <= i < B_TILES:
-                keep_h(i)
-            if 0 <= b - 1 < B_TILES:
-                sigmoid(b - 1, 0)
+            if CHUNK <= i < CHUNK + B_TILES:
+                keep_h(i - CHUNK)
             if 0 <= b - 1 < B_TILES:
                 sigmoid(b - 1, 1)
             if 0 <= b - 3 < B_TILES:
@@ -294,20 +293,19 @@ def tile_liquidmemorycell_pb_k_kernel(tc, x, h, h_candidate, Wd, bd, Wu, bu, out
                     out=candidate[:].rearrange("p b n -> p (b n)"),
                     in_=h_candidate.rearrange("(p b) n -> p (b n)", b=B_TILES),
                 )
-            if i == AHEAD:
-                spread_biases()
+            if i == 2 * CHUNK:
                 prepare_epilogue()
-            if 0 <= b - 1 < B_TILES:
-                blend_step(b - 1, 0)
             if 0 <= i < UNITS:
                 quantise_unit(i)
-            if 0 <= b - 1 < B_TILES:
-                blend_step(b - 1, 1)
-            if 0 <= b - 0 < B_TILES:
-                add_bias(b - 0, 0)
+            if 0 <= b < B_TILES:
+                add_bias(b, 0)
+                sigmoid(b, 0)
             if 0 <= b - 1 < B_TILES:
                 blend_step(b - 1, 2)
-            if 0 <= b - 0 < B_TILES:
-                add_bias(b - 0, 1)
+            if 0 <= b < B_TILES:
+                add_bias(b, 1)
             if 0 <= b - 1 < B_TILES:
                 blend_step(b - 1, 3)
+            if 0 <= b < B_TILES:
+                blend_step(b, 0)
+                blend_step(b, 1)

import math
from contextlib import ExitStack

import concourse.mybir as mybir
from concourse.masks import make_identity

F32 = mybir.dt.float32
BF16 = mybir.dt.bfloat16
U32 = mybir.dt.uint32
U8 = mybir.dt.uint8
FP8X4 = mybir.dt.float8_e4m3fn_x4
ALU = mybir.AluOpType
ACT = mybir.ActivationFunctionType

BATCH, IN_DIM, MEM = 512, 16128, 256
K = MEM + IN_DIM
P = 128
PACK = 4
K_PASS = P * PACK
PASSES = K // K_PASS
B_TILES = BATCH // P
N_OUT = 2 * MEM
BANK_WORDS = 512

CHUNK = 4
UNIT_COLS = CHUNK * K_PASS
UNITS = (PASSES // CHUNK) * B_TILES
TRANSPOSES_PER_BANK = BANK_WORDS // P
BANKS_PER_UNIT = 2 * CHUNK // TRANSPOSES_PER_BANK

W_LEAD = 3
AHEAD = 6
C_BUFS = AHEAD
W_BUFS = (AHEAD + 2) // 2
STAGE_BUFS = 3
V_COLS = 160
RUN = 4

MIN_TS, MAX_TS, EPS = 0.1, 10.0, 1e-6
SPAN = MAX_TS - MIN_TS
DECAY_LO = MIN_TS + EPS
DECAY_HI = DECAY_LO + SPAN
INV_HI = 1.0 / DECAY_HI
INV_SPAN = SPAN / (DECAY_LO * DECAY_HI)
S_ADD = INV_HI / INV_SPAN
SHIFT = math.log(DECAY_HI / DECAY_LO)
H_SQ_FLOOR = 1e-12
M_SQ_FLOOR = 1e-24

FLOPS = 2 * BATCH * K * N_OUT


def tile_liquidmemorycell_pb_k_kernel(tc, x, h, h_candidate, Wd, bd, Wu, bu, out):
    nc = tc.nc
    weights = (Wd, Wu)
    x_tiles = x.rearrange("(p b) k -> p b k", b=B_TILES)
    out_tiles = out.rearrange("(p b) n -> p b n", b=B_TILES)
    with ExitStack() as ctx:
        consts = ctx.enter_context(tc.tile_pool(name="consts", bufs=1))
        c_pool = ctx.enter_context(tc.tile_pool(name="c_rows", bufs=C_BUFS))
        w_pool = ctx.enter_context(tc.tile_pool(name="w_rows", bufs=W_BUFS))
        grouped = ctx.enter_context(tc.tile_pool(name="grouped", bufs=STAGE_BUFS))
        w_mx = ctx.enter_context(tc.tile_pool(name="w_mx", bufs=W_LEAD + CHUNK + 1))
        c_mx = ctx.enter_context(tc.tile_pool(name="c_mx", bufs=STAGE_BUFS))
        tail = ctx.enter_context(tc.tile_pool(name="tail", bufs=4))
        sums_pool = ctx.enter_context(tc.psum_pool(name="sums", bufs=1))
        planes_pool = ctx.enter_context(tc.psum_pool(name="planes", bufs=2 * BANKS_PER_UNIT))
        ctx.enter_context(tc.manual_schedule())

        c_rows, c_planes, c_grouped, c_codes, c_scales = {}, {}, {}, {}, {}
        w_rows, w_grouped, w_codes, w_scales = {}, {}, {}, {}
        biased, gates, blends, ratios = {}, {}, {}, {}

        def load_unit(n):
            chunk, b = divmod(n, B_TILES)
            rows = c_pool.tile([P, UNIT_COLS], BF16, name="c_rows")
            if chunk == 0:
                nc.sync.dma_start(out=rows[:, MEM:], in_=x_tiles[:, b, 0 : UNIT_COLS - MEM])
            else:
                first = chunk * UNIT_COLS - MEM
                nc.sync.dma_start(out=rows[:], in_=x_tiles[:, b, first : first + UNIT_COLS])
            c_rows[n] = rows

        def load_weight_pair(q):
            k_rows = slice(2 * q * K_PASS, (2 * q + 2) * K_PASS)
            rows = w_pool.tile([P, 2, 2, PACK, MEM], BF16, name="w_rows")
            for w in range(2):
                nc.sync.dma_start(
                    out=rows[:, w].rearrange("p g t n -> p g (t n)"),
                    in_=weights[w][k_rows, :].rearrange("(g p t) n -> p g (t n)", g=2, t=PACK),
                )
            w_rows[q] = rows

        def load_round(j):
            load_unit(j)
            if (j + W_LEAD) % 2 == 0 and j + W_LEAD < PASSES:
                load_weight_pair((j + W_LEAD) // 2)

        def regroup_weights(g):
            rows = w_rows[g // 2]
            side = grouped.tile([P, 2, MEM, PACK], BF16, name="w_grouped", align_bytes=64)
            nc.vector.tensor_copy(
                out=side[:, :, 0:V_COLS, :].rearrange("p w (c i) t -> p w c t i", i=RUN),
                in_=rows[:, :, g % 2, :, 0:V_COLS].rearrange("p w t (c i) -> p w c t i", i=RUN),
            )
            for w in range(2):
                nc.scalar.copy(
                    out=side[:, w, V_COLS:, :].rearrange("p (c i) t -> p c t i", i=RUN),
                    in_=rows[:, w, g % 2, :, V_COLS:].rearrange("p t (c i) -> p c t i", i=RUN),
                )
            w_grouped[g] = side

        def quantise_weights(g):
            codes = w_mx.tile([P, N_OUT], U32, name="w_codes", align_bytes=64)
            scales = w_mx.tile([P, N_OUT], U8, name="w_scales", align_bytes=64)
            nc.vector.quantize_mx(
                out=codes[:].bitcast(FP8X4),
                scales=scales[:],
                in_=w_grouped[g][:].rearrange("p w n t -> p (w n t)"),
            )
            w_codes[g], w_scales[g] = codes, scales

        def transpose_unit(n):
            words = c_rows[n][:].bitcast(F32)
            planes = words.rearrange("r (g p u) -> r g u p", g=CHUNK, u=2)
            banks = []
            for f in range(BANKS_PER_UNIT):
                bank = planes_pool.tile([P, TRANSPOSES_PER_BANK, P], F32, name="planes")
                for j in range(TRANSPOSES_PER_BANK):
                    g, u = divmod(f * TRANSPOSES_PER_BANK + j, 2)
                    nc.tensor.transpose(bank[:, j, :], planes[:, g, u, :], identity[:])
                banks.append(bank)
            c_planes[n] = banks

        def copy_out_unit(n):
            side = grouped.tile([P, UNIT_COLS], BF16, name="c_grouped", align_bytes=64)
            side_words = side[:].bitcast(F32).rearrange("p (f g r u) -> p f g r u", f=BANKS_PER_UNIT, r=P, u=2)
            for f in range(BANKS_PER_UNIT):
                nc.scalar.copy(
                    out=side_words[:, f],
                    in_=c_planes[n][f][:].rearrange("p (g u) r -> p g r u", u=2),
                )
            c_grouped[n] = side

        def quantise_unit(n):
            codes = c_mx.tile([P, CHUNK * P], U32, name="c_codes", align_bytes=64)
            scales = c_mx.tile([P, CHUNK * P], U8, name="c_scales", align_bytes=64)
            nc.vector.quantize_mx(out=codes[:].bitcast(FP8X4), scales=scales[:], in_=c_grouped[n][:])
            c_codes[n], c_scales[n] = codes, scales

        def multiply_unit(n):
            chunk, b = divmod(n, B_TILES)
            for j in range(CHUNK):
                g = chunk * CHUNK + j
                cols = slice(j * P, (j + 1) * P)
                nc.tensor.matmul_mx(
                    out=sums[b][:],
                    lhsT=c_codes[n][:, cols].bitcast(FP8X4),
                    lhsT_scale=c_scales[n][:, cols],
                    rhs=w_codes[g][:].bitcast(FP8X4),
                    rhs_scale=w_scales[g][:],
                    start=(g == 0),
                    stop=(g == PASSES - 1),
                )

        def keep_h(b):
            h_cols = h_rows[:, b, :]
            squares = tail.tile([P, MEM], F32, name="squares")
            nc.scalar.activation(out=h_span[:, b, :], in_=h_cols, func=ACT.Copy, scale=INV_SPAN)
            nc.scalar.activation(out=squares[:], in_=h_cols, func=ACT.Square, accum_out=h_sq[:, b : b + 1])

        def prepare_epilogue():
            nc.gpsimd.tensor_scalar(out=inv_h_sq[:], in0=h_sq[:], scalar1=H_SQ_FLOOR, scalar2=None, op0=ALU.max)
            nc.gpsimd.tensor_tensor(out=inv_h_sq[:], in0=inv_h_sq[:], in1=minus_one[:], op=ALU.pow)

        def spread_biases():
            bias_bank = planes_pool.tile([P, N_OUT], F32, name="planes")
            nc.tensor.matmul(out=bias_bank[:], lhsT=ones[:], rhs=bias_row[:], start=True, stop=True)
            nc.scalar.activation(out=bias_all[:, 0:MEM], in_=bias_bank[:, 0:MEM], func=ACT.Identity, bias=SHIFT)
            nc.scalar.copy(out=bias_all[:, MEM:], in_=bias_bank[:, MEM:])

        def add_bias(b, k):
            if k == 0:
                biased[b] = tail.tile([P, N_OUT], F32, name="biased")
            cols = slice(k * MEM, (k + 1) * MEM)
            nc.vector.tensor_tensor(out=biased[b][:, cols], in0=sums[b][:, cols], in1=bias_all[:, cols], op=ALU.add)

        def sigmoid(b, k):
            if k == 0:
                gates[b] = tail.tile([P, N_OUT], F32, name="gate")
            cols = slice(k * MEM, (k + 1) * MEM)
            nc.scalar.activation(out=gates[b][:, cols], in_=biased[b][:, cols], func=ACT.Sigmoid, scale=-1.0)

        def blend_step(b, step):
            gate = gates[b]
            if step == 0:
                blends[b] = tail.tile([P, MEM], F32, name="m")
            m = blends[b]
            if step == 0:
                nc.vector.scalar_tensor_tensor(
                    out=m[:], in0=gate[:, 0:MEM], scalar=S_ADD, in1=h_span[:, b, :], op0=ALU.add, op1=ALU.mult
                )
            elif step == 1:
                nc.vector.tensor_tensor(out=m[:], in0=m[:], in1=candidate[:, b, :], op=ALU.subtract)
            elif step == 2:
                nc.vector.tensor_tensor(out=m[:], in0=m[:], in1=gate[:, MEM:], op=ALU.mult)
            else:
                nc.vector.tensor_tensor(out=m[:], in0=m[:], in1=candidate[:, b, :], op=ALU.add)

        def norm_ratio(b):
            squares = tail.tile([P, MEM], F32, name="squares")
            m_sq = tail.tile([P, 1], F32, name="m_sq")
            nc.scalar.activation(out=squares[:], in_=blends[b][:], func=ACT.Square, accum_out=m_sq[:])
            ratio = tail.tile([P, 1], F32, name="ratio")
            nc.gpsimd.tensor_scalar(
                out=ratio[:], in0=m_sq[:], scalar1=M_SQ_FLOOR, scalar2=inv_h_sq[:, b : b + 1], op0=ALU.max, op1=ALU.mult
            )
            nc.gpsimd.tensor_tensor(out=ratio[:], in0=ratio[:], in1=minus_half[:], op=ALU.pow)
            ratios[b] = ratio

        def store_tile(b):
            result = tail.tile([P, MEM], F32, name="result")
            nc.scalar.activation(out=result[:], in_=blends[b][:], func=ACT.Copy, scale=ratios[b][:])
            nc.sync.dma_start(out=out_tiles[:, b, :], in_=result[:])

        identity = consts.tile([P, P], F32, name="identity")
        make_identity(nc, identity[:])
        minus_one = consts.tile([P, B_TILES], F32, name="minus_one")
        nc.gpsimd.memset(minus_one[:], -1.0)
        minus_half = consts.tile([P, 1], F32, name="minus_half")
        nc.gpsimd.memset(minus_half[:], -0.5)

        ones = consts.tile([P, P], BF16, name="ones")
        nc.vector.memset(ones[:], 1.0)
        bias_row = consts.tile([P, N_OUT], BF16, name="bias_row")
        nc.vector.memset(bias_row[:], 0.0)
        warm = consts.tile([P, 1], F32, name="warm")
        nc.vector.memset(warm[:], 0.0)
        nc.scalar.activation(out=warm[:], in_=warm[:], func=ACT.Sigmoid)

        h_rows = consts.tile([P, B_TILES, MEM], BF16, name="h_rows")
        load_weight_pair(0)
        nc.sync.dma_start(
            out=h_rows[:].rearrange("p b n -> p (b n)"), in_=h.rearrange("(p b) n -> p (b n)", b=B_TILES)
        )
        nc.sync.dma_start(out=bias_row[0:1, 0:MEM], in_=bd.rearrange("(o n) -> o n", o=1))
        nc.sync.dma_start(out=bias_row[0:1, MEM:], in_=bu.rearrange("(o n) -> o n", o=1))
        load_round(0)
        load_weight_pair(1)
        for j in range(1, AHEAD):
            load_round(j)
        candidate = consts.tile([P, B_TILES, MEM], BF16, name="candidate")

        bias_all = consts.tile([P, N_OUT], F32, name="bias_all")

        h_span = consts.tile([P, B_TILES, MEM], F32, name="h_span")
        h_sq = consts.tile([P, B_TILES], F32, name="h_sq")
        inv_h_sq = consts.tile([P, B_TILES], F32, name="inv_h_sq")
        sums = []
        for b in range(B_TILES):
            bank = sums_pool.tile([P, N_OUT], F32, name="sums%d" % b)
            sums.append(bank)

        for i in range(-W_LEAD, UNITS + 5):
            g = i + W_LEAD
            b = i - 1 - (UNITS - B_TILES)
            if 1 <= g <= PASSES:
                quantise_weights(g - 1)
            if i == -1:
                for n in range(B_TILES):
                    nc.scalar.copy(out=c_rows[n][:, 0:MEM], in_=h_rows[:, n, :])
                spread_biases()
            if 0 <= i < UNITS:
                transpose_unit(i)
            if 1 <= i <= UNITS:
                multiply_unit(i - 1)
            if 0 <= i < UNITS:
                copy_out_unit(i)
            if CHUNK <= i < CHUNK + B_TILES:
                keep_h(i - CHUNK)
            if 0 <= b - 1 < B_TILES:
                sigmoid(b - 1, 1)
            if 0 <= b - 3 < B_TILES:
                store_tile(b - 3)
            if 0 <= b - 2 < B_TILES:
                norm_ratio(b - 2)
            if g < PASSES:
                regroup_weights(g)
            if 0 <= i and i + AHEAD < UNITS:
                load_round(i + AHEAD)
            if i + AHEAD == UNITS:
                nc.sync.dma_start(
                    out=candidate[:].rearrange("p b n -> p (b n)"),
                    in_=h_candidate.rearrange("(p b) n -> p (b n)", b=B_TILES),
                )
            if i == 2 * CHUNK:
                prepare_epilogue()
            if 0 <= i < UNITS:
                quantise_unit(i)
            if 0 <= b < B_TILES:
                add_bias(b, 0)
                sigmoid(b, 0)
            if 0 <= b - 1 < B_TILES:
                blend_step(b - 1, 2)
            if 0 <= b < B_TILES:
                add_bias(b, 1)
            if 0 <= b - 1 < B_TILES:
                blend_step(b - 1, 3)
            if 0 <= b < B_TILES:
                blend_step(b, 0)
                blend_step(b, 1)
